import numpy as np
import ml_dtypes


def mxq(x, axis, fmt="e4m3"):
    dtype, down = {"e4m3": (ml_dtypes.float8_e4m3fn, 7), "e5m2": (ml_dtypes.float8_e5m2, 14)}[fmt]
    v = np.moveaxis(np.asarray(x, np.float32).astype(ml_dtypes.bfloat16).astype(np.float64), axis, -1)
    blocks = v.reshape(v.shape[:-1] + (-1, 32))
    amax = np.abs(blocks).max(-1, keepdims=True)
    byte = np.maximum(np.where(amax > 0, np.frexp(amax)[1] - 1 + 127, 0) - down, 1)
    scale = np.exp2(byte - 127.0)
    codes = (blocks / scale).astype(np.float32).astype(dtype).astype(np.float64)
    return np.moveaxis((codes * scale).reshape(v.shape), -1, axis)


WIDE = False


def mx_kscale(k):
    if not WIDE:
        return np.ones(k)
    levels = np.array([10, -10, 5, -5, 0])
    a = np.random.permutation(np.resize(levels, k // 512 * 4)).reshape(k // 512, 4)
    idx = np.arange(k)
    return np.exp2(a[idx // 512, idx % 128 // 32])


BF16 = ml_dtypes.bfloat16


def bf(x):
    return np.asarray(x, np.float32).astype(BF16)


def f64(x):
    return np.asarray(x).astype(np.float64)


B, S, D, H, HD = 8, 512, 1024, 4, 128
I = H * HD


def silu(v):
    return v / (1.0 + np.exp(-v))


def setup_inputs():
    t = mx_kscale(I)
    h = silu(np.random.standard_normal((B, S, I))) * np.random.standard_normal((B, S, I))
    return {"h_inter": bf(h * t),
            "adjacency": bf(np.random.uniform(size=(B, H, S, S)) * 2.0 / np.sqrt(S)),
            "Wd": bf(np.random.standard_normal((I, D)) / np.sqrt(I) / t[:, None]),
            "eps": bf(np.random.standard_normal(H) * 0.2),
            "alpha": bf(1.0 + np.random.standard_normal(H) * 0.2)}


def reference(h_inter, adjacency, Wd, eps, alpha):
    h_heads = f64(h_inter).reshape(B, S, H, HD).transpose(0, 2, 1, 3)
    agg = mxq(f64(adjacency), 3, "e4m3") @ mxq(h_heads, 2, "e4m3")
    e = (1.0 + f64(eps))[None, :, None, None]
    a = f64(alpha)[None, :, None, None]
    h_gin = e * h_heads + a * agg
    h_comb = h_gin.transpose(0, 2, 1, 3).reshape(B, S, I)
    return mxq(h_comb, 2, "e4m3") @ mxq(f64(Wd), 0, "e4m3")

@@ -1,0 +1,279 @@
+from contextlib import ExitStack
+
+import concourse.mybir as mybir
+from concourse.masks import make_identity
+
+BF16 = mybir.dt.bfloat16
+F32 = mybir.dt.float32
+U32 = mybir.dt.uint32
+U8 = mybir.dt.uint8
+FP8X4 = mybir.dt.float8_e4m3fn_x4
+MULT = mybir.AluOpType.mult
+ADD = mybir.AluOpType.add
+
+B, S, I, H, HD, D = 8, 512, 512, 4, 128, 1024
+P = 128
+PACK = 4
+BANK = 512
+HALVES = 2
+
+FLOPS = 2 * B * H * S * S * HD + 2 * B * S * I * D
+
+STEPS = B * H
+PREFETCH = 12
+G_LAG = 5
+WD_PIECES = 4
+WD_FIRST_STEP = 1
+
+
+def tile_llamamlp_halfwaygin_pa_t_kernel(tc, h_inter, adjacency, Wd, eps, alpha, out):
+    nc = tc.nc
+    with ExitStack() as ctx:
+        ctx.enter_context(tc.manual_schedule())
+        consts = ctx.enter_context(tc.tile_pool(name="consts", bufs=1))
+        a_pool = ctx.enter_context(tc.tile_pool(name="a_pool", bufs=PREFETCH + 1))
+        h_pool = ctx.enter_context(tc.tile_pool(name="h_pool", bufs=PREFETCH // H + 2))
+        work = ctx.enter_context(tc.tile_pool(name="work", bufs=3))
+        out_pool = ctx.enter_context(tc.tile_pool(name="out_pool", bufs=3))
+        psum_t = ctx.enter_context(tc.psum_pool(name="psum_t", bufs=3))
+        psum_agg = ctx.enter_context(tc.psum_pool(name="psum_agg", bufs=2))
+        psum_out = ctx.enter_context(tc.psum_pool(name="psum_out", bufs=3))
+
+        a_raw_of, h_raw_of = {}, {}
+        a_codes_of, h_codes_of, g_codes_of = {}, {}, {}
+        h_grouped_of, h_scaled_of, g_of, g_grouped_of, wd_grouped_of, out_of = {}, {}, {}, {}, {}, {}
+
+        def live(step):
+            return 0 <= step < STEPS
+
+        def in_place_order(rows):
+            return rows.rearrange("(u p e) w -> p u (e w)", u=HALVES, e=2)
+
+        def load(tile, rows):
+            nc.sync.dma_start(
+                out=tile[:].rearrange("p (u e) w -> p u (e w)", u=HALVES), in_=in_place_order(rows)
+            )
+
+        def load_step(s):
+            b, n = divmod(s, H)
+            a_raw = a_pool.tile([P, PACK, S], BF16)
+            load(a_raw, adjacency[b, n])
+            a_raw_of[s] = a_raw
+            if n == 0:
+                h_raw = h_pool.tile([P, PACK, I], BF16)
+                load(h_raw, h_inter[b])
+                h_raw_of[b] = h_raw
+
+        def head_columns(s):
+            n = s % H
+            return slice(n * HD, (n + 1) * HD)
+
+        def regroup(engine_copy, grouped, raw):
+            engine_copy(
+                out=grouped.rearrange("p (c i) t -> p c t i", i=4),
+                in_=raw.rearrange("p t (c i) -> p c t i", i=4),
+            )
+
+        def h_regroup(s):
+            h_grouped = work.tile([P, HD, PACK], BF16, align_bytes=64)
+            regroup(nc.vector.tensor_copy, h_grouped[:], h_raw_of[s // H][:, :, head_columns(s)])
+            h_grouped_of[s] = h_grouped
+
+        def h_scale(s):
+            h_scaled = work.tile([P, PACK, HD], F32)
+            nc.vector.tensor_scalar(
+                out=h_scaled[:],
+                in0=h_raw_of[s // H][:, :, head_columns(s)],
+                scalar1=one_plus_eps[:, s % H : s % H + 1],
+                scalar2=None,
+                op0=MULT,
+            )
+            h_scaled_of[s] = h_scaled
+
+        def quantise(grouped, codes, scales):
+            nc.vector.quantize_mx(
+                out=codes.bitcast(FP8X4), scales=scales, in_=grouped.rearrange("p c t -> p (c t)")
+            )
+
+        def h_quantise(s):
+            h_codes = work.tile([P, HD], U32, align_bytes=64)
+            h_scales = work.tile([P, HD], U8, align_bytes=64)
+            quantise(h_grouped_of[s][:], h_codes[:], h_scales[:])
+            h_codes_of[s] = (h_codes, h_scales)
+
+        def transpose_row_set(bank_part, raw, t):
+            words = raw[:].bitcast(F32)
+            for u in range(HALVES):
+                nc.tensor.transpose(bank_part[:, u, :], words[:, t, u * P : (u + 1) * P], ident[:])
+
+        def a_transpose_and_copy(s):
+            a_raw = a_raw_of[s]
+            a_grouped = work.tile([P, S, PACK], BF16, align_bytes=64)
+            a_words = a_grouped[:].bitcast(F32)
+            sets_a_bank = BANK // (HALVES * P)
+            banks = []
+            for first_set in range(0, PACK, sets_a_bank):
+                a_bank = psum_t.tile([P, HALVES, sets_a_bank, P], F32, tag="transposed")
+                for i in range(sets_a_bank):
+                    transpose_row_set(a_bank[:, :, i, :], a_raw, first_set + i)
+                banks.append((first_set, a_bank))
+            for first_set, a_bank in banks:
+                nc.scalar.copy(
+                    out=a_words[:, first_set * P : (first_set + sets_a_bank) * P, :],
+                    in_=a_bank[:].rearrange("q u i p -> q (i p) u"),
+                )
+            return a_grouped
+
+        def a_quantise(s, a_grouped):
+            a_codes = work.tile([P, S], U32, align_bytes=64)
+            a_scales = work.tile([P, S], U8, align_bytes=64)
+            quantise(a_grouped[:], a_codes[:], a_scales[:])
+            a_codes_of[s] = (a_codes, a_scales)
+
+        def first_matmul(s):
+            a_codes, a_scales = a_codes_of[s]
+            h_codes, h_scales = h_codes_of[s]
+            agg = psum_agg.tile([P, PACK, HD], F32)
+            for t in range(PACK):
+                row_set = slice(t * P, (t + 1) * P)
+                nc.tensor.matmul_mx(
+                    out=agg[:, t, :],
+                    lhsT=a_codes[:, row_set].bitcast(FP8X4),
+                    lhsT_scale=a_scales[:, row_set],
+                    rhs=h_codes[:].bitcast(FP8X4),
+                    rhs_scale=h_scales[:],
+                    start=True,
+                    stop=True,
+                )
+            return agg
+
+        def combine(s, agg):
+            b, n = divmod(s, H)
+            if n == 0:
+                g_new = work.tile([P, PACK, I], BF16)
+                g_of[b] = g_new
+            nc.vector.scalar_tensor_tensor(
+                out=g_of[b][:, :, head_columns(s)],
+                in0=agg[:],
+                scalar=alpha_f32[:, n : n + 1],
+                in1=h_scaled_of[s][:],
+                op0=MULT,
+                op1=ADD,
+            )
+
+        def g_transpose(j):
+            b, t = divmod(j, PACK)
+            g_bank = psum_t.tile([P, HALVES, P], F32, tag="transposed")
+            transpose_row_set(g_bank[:], g_of[b], t)
+            return g_bank
+
+        def g_copy(j, g_bank):
+            g_grouped = work.tile([P, P, PACK], BF16, align_bytes=64)
+            nc.vector.tensor_copy(
+                out=g_grouped[:].bitcast(F32), in_=g_bank[:].rearrange("q u p -> q p u")
+            )
+            g_grouped_of[j] = g_grouped
+
+        def g_quantise(j):
+            g_codes = work.tile([P, P], U32, align_bytes=64)
+            g_scales = work.tile([P, P], U8, align_bytes=64)
+            quantise(g_grouped_of[j][:], g_codes[:], g_scales[:])
+            g_codes_of[j] = (g_codes, g_scales)
+
+        def wd_columns(piece):
+            return slice(piece * (D // WD_PIECES), (piece + 1) * (D // WD_PIECES))
+
+        def wd_regroup(piece):
+            wd_grouped = work.tile([P, D // WD_PIECES, PACK], BF16, align_bytes=64)
+            regroup(nc.scalar.copy, wd_grouped[:], wd_raw[:, :, wd_columns(piece)])
+            wd_grouped_of[piece] = wd_grouped
+
+        def wd_quantise(piece):
+            quantise(
+                wd_grouped_of[piece][:],
+                wd_codes[:, wd_columns(piece)],
+                wd_scales[:, wd_columns(piece)],
+            )
+
+        def second_matmul_and_store(j):
+            b, t = divmod(j, PACK)
+            u, e = divmod(t, 2)
+            g_codes, g_scales = g_codes_of[j]
+            if e == 0:
+                out_new = out_pool.tile([P, 2, D], F32)
+                out_of[(b, u)] = out_new
+            out_sb = out_of[(b, u)]
+            banks = []
+            for d0 in range(0, D, BANK):
+                out_bank = psum_out.tile([P, BANK], F32)
+                nc.tensor.matmul_mx(
+                    out=out_bank[:],
+                    lhsT=g_codes[:].bitcast(FP8X4),
+                    lhsT_scale=g_scales[:],
+                    rhs=wd_codes[:, d0 : d0 + BANK].bitcast(FP8X4),
+                    rhs_scale=wd_scales[:, d0 : d0 + BANK],
+                    start=True,
+                    stop=True,
+                )
+                banks.append((d0, out_bank))
+            for d0, out_bank in banks:
+                nc.scalar.copy(out=out_sb[:, e, d0 : d0 + BANK], in_=out_bank[:])
+            if e == 1:
+                nc.scalar.dma_start(
+                    out=out[b, u * 2 * P : (u + 1) * 2 * P, :].rearrange("(p e) d -> p (e d)", e=2),
+                    in_=out_sb[:].rearrange("p e d -> p (e d)"),
+                )
+
+        load_step(0)
+        load_step(1)
+        wd_raw = consts.tile([P, PACK, D], BF16)
+        load(wd_raw, Wd)
+        for s in range(2, PREFETCH):
+            load_step(s)
+
+        ident = consts.tile([P, P], F32)
+        make_identity(nc, ident[:])
+        eps_bf16 = consts.tile([P, H], BF16)
+        alpha_bf16 = consts.tile([P, H], BF16)
+        nc.scalar.dma_start(out=eps_bf16[:], in_=eps.partition_broadcast(P))
+        nc.scalar.dma_start(out=alpha_bf16[:], in_=alpha.partition_broadcast(P))
+        one_plus_eps = consts.tile([P, H], F32)
+        alpha_f32 = consts.tile([P, H], F32)
+        nc.vector.tensor_scalar_add(out=one_plus_eps[:], in0=eps_bf16[:], scalar1=1.0)
+        nc.vector.tensor_copy(out=alpha_f32[:], in_=alpha_bf16[:])
+        wd_codes = consts.tile([P, D], U32, align_bytes=64)
+        wd_scales = consts.tile([P, D], U8, align_bytes=64)
+
+        h_regroup(0)
+        h_scale(0)
+        h_quantise(0)
+
+        for s in range(STEPS + G_LAG + 1):
+            j = s - G_LAG
+            piece = s - WD_FIRST_STEP
+            if live(s + PREFETCH):
+                load_step(s + PREFETCH)
+            if live(s):
+                a_grouped = a_transpose_and_copy(s)
+            if live(j):
+                g_bank = g_transpose(j)
+                g_copy(j, g_bank)
+            if 0 <= piece < WD_PIECES:
+                wd_regroup(piece)
+            if live(s + 1):
+                h_regroup(s + 1)
+            if live(s):
+                a_quantise(s, a_grouped)
+            if live(s + 1):
+                h_scale(s + 1)
+            if live(j):
+                g_quantise(j)
+            if 0 <= piece - 1 < WD_PIECES:
+                wd_quantise(piece - 1)
+            if live(s - 1):
+                agg = first_matmul(s - 1)
+                combine(s - 1, agg)
+            if live(s + 1):
+                h_quantise(s + 1)
+            if live(j - 1):
+                second_matmul_and_store(j - 1)

@@ -24,6 +24,7 @@ PREFETCH = 12
 G_LAG = 5
 WD_PIECES = 4
 WD_FIRST_STEP = 1
+OUT_PASS_REPEATS = 2
 
 
 def tile_llamamlp_halfwaygin_pa_t_kernel(tc, h_inter, adjacency, Wd, eps, alpha, out):
@@ -206,15 +207,16 @@ def tile_llamamlp_halfwaygin_pa_t_kernel(tc, h_inter, adjacency, Wd, eps, alpha,
             banks = []
             for d0 in range(0, D, BANK):
                 out_bank = psum_out.tile([P, BANK], F32)
-                nc.tensor.matmul_mx(
-                    out=out_bank[:],
-                    lhsT=g_codes[:].bitcast(FP8X4),
-                    lhsT_scale=g_scales[:],
-                    rhs=wd_codes[:, d0 : d0 + BANK].bitcast(FP8X4),
-                    rhs_scale=wd_scales[:, d0 : d0 + BANK],
-                    start=True,
-                    stop=True,
-                )
+                for repeat in range(OUT_PASS_REPEATS):
+                    nc.tensor.matmul_mx(
+                        out=out_bank[:],
+                        lhsT=g_codes[:].bitcast(FP8X4),
+                        lhsT_scale=g_scales[:],
+                        rhs=wd_codes[:, d0 : d0 + BANK].bitcast(FP8X4),
+                        rhs_scale=wd_scales[:, d0 : d0 + BANK],
+                        start=True,
+                        stop=True,
+                    )
                 banks.append((d0, out_bank))
             for d0, out_bank in banks:
                 nc.scalar.copy(out=out_sb[:, e, d0 : d0 + BANK], in_=out_bank[:])

@@ -21,10 +21,9 @@ FLOPS = 2 * B * H * S * S * HD + 2 * B * S * I * D
 
 STEPS = B * H
 PREFETCH = 12
-G_LAG = 5
+G_LAG = 6
 WD_PIECES = 4
 WD_FIRST_STEP = 1
-OUT_PASS_REPEATS = 2
 
 
 def tile_llamamlp_halfwaygin_pa_t_kernel(tc, h_inter, adjacency, Wd, eps, alpha, out):
@@ -207,16 +206,15 @@ def tile_llamamlp_halfwaygin_pa_t_kernel(tc, h_inter, adjacency, Wd, eps, alpha,
             banks = []
             for d0 in range(0, D, BANK):
                 out_bank = psum_out.tile([P, BANK], F32)
-                for repeat in range(OUT_PASS_REPEATS):
-                    nc.tensor.matmul_mx(
-                        out=out_bank[:],
-                        lhsT=g_codes[:].bitcast(FP8X4),
-                        lhsT_scale=g_scales[:],
-                        rhs=wd_codes[:, d0 : d0 + BANK].bitcast(FP8X4),
-                        rhs_scale=wd_scales[:, d0 : d0 + BANK],
-                        start=True,
-                        stop=True,
-                    )
+                nc.tensor.matmul_mx(
+                    out=out_bank[:],
+                    lhsT=g_codes[:].bitcast(FP8X4),
+                    lhsT_scale=g_scales[:],
+                    rhs=wd_codes[:, d0 : d0 + BANK].bitcast(FP8X4),
+                    rhs_scale=wd_scales[:, d0 : d0 + BANK],
+                    start=True,
+                    stop=True,
+                )
                 banks.append((d0, out_bank))
             for d0, out_bank in banks:
                 nc.scalar.copy(out=out_sb[:, e, d0 : d0 + BANK], in_=out_bank[:])

@@ -23,7 +23,7 @@ STEPS = B * H
 PREFETCH = 12
 G_LAG = 6
 WD_PIECES = 4
-WD_FIRST_STEP = 1
+WD_FIRST_STEP = 2
 
 
 def tile_llamamlp_halfwaygin_pa_t_kernel(tc, h_inter, adjacency, Wd, eps, alpha, out):
@@ -34,14 +34,15 @@ def tile_llamamlp_halfwaygin_pa_t_kernel(tc, h_inter, adjacency, Wd, eps, alpha,
         a_pool = ctx.enter_context(tc.tile_pool(name="a_pool", bufs=PREFETCH + 1))
         h_pool = ctx.enter_context(tc.tile_pool(name="h_pool", bufs=PREFETCH // H + 2))
         work = ctx.enter_context(tc.tile_pool(name="work", bufs=3))
-        out_pool = ctx.enter_context(tc.tile_pool(name="out_pool", bufs=3))
+        scaled_pool = ctx.enter_context(tc.tile_pool(name="scaled_pool", bufs=PREFETCH + H))
+        out_pool = ctx.enter_context(tc.tile_pool(name="out_pool", bufs=6))
         psum_t = ctx.enter_context(tc.psum_pool(name="psum_t", bufs=3))
         psum_agg = ctx.enter_context(tc.psum_pool(name="psum_agg", bufs=2))
         psum_out = ctx.enter_context(tc.psum_pool(name="psum_out", bufs=3))
 
         a_raw_of, h_raw_of = {}, {}
         a_codes_of, h_codes_of, g_codes_of = {}, {}, {}
-        h_grouped_of, h_scaled_of, g_of, g_grouped_of, wd_grouped_of, out_of = {}, {}, {}, {}, {}, {}
+        h_grouped_of, h_scaled_of, agg_of, g_of, g_grouped_of, wd_grouped_of = {}, {}, {}, {}, {}, {}
 
         def live(step):
             return 0 <= step < STEPS
@@ -80,13 +81,14 @@ def tile_llamamlp_halfwaygin_pa_t_kernel(tc, h_inter, adjacency, Wd, eps, alpha,
             h_grouped_of[s] = h_grouped
 
         def h_scale(s):
-            h_scaled = work.tile([P, PACK, HD], F32)
-            nc.vector.tensor_scalar(
+            h_scaled = scaled_pool.tile([P, PACK, HD], F32)
+            nc.gpsimd.tensor_scalar(
                 out=h_scaled[:],
                 in0=h_raw_of[s // H][:, :, head_columns(s)],
                 scalar1=one_plus_eps[:, s % H : s % H + 1],
-                scalar2=None,
+                scalar2=0.0,
                 op0=MULT,
+                op1=ADD,
             )
             h_scaled_of[s] = h_scaled
 
@@ -145,16 +147,16 @@ def tile_llamamlp_halfwaygin_pa_t_kernel(tc, h_inter, adjacency, Wd, eps, alpha,
                     start=True,
                     stop=True,
                 )
-            return agg
+            agg_of[s] = agg
 
-        def combine(s, agg):
+        def combine(s):
             b, n = divmod(s, H)
             if n == 0:
                 g_new = work.tile([P, PACK, I], BF16)
                 g_of[b] = g_new
             nc.vector.scalar_tensor_tensor(
                 out=g_of[b][:, :, head_columns(s)],
-                in0=agg[:],
+                in0=agg_of[s][:],
                 scalar=alpha_f32[:, n : n + 1],
                 in1=h_scaled_of[s][:],
                 op0=MULT,
@@ -199,10 +201,7 @@ def tile_llamamlp_halfwaygin_pa_t_kernel(tc, h_inter, adjacency, Wd, eps, alpha,
             b, t = divmod(j, PACK)
             u, e = divmod(t, 2)
             g_codes, g_scales = g_codes_of[j]
-            if e == 0:
-                out_new = out_pool.tile([P, 2, D], F32)
-                out_of[(b, u)] = out_new
-            out_sb = out_of[(b, u)]
+            out_sb = out_pool.tile([P, D], F32)
             banks = []
             for d0 in range(0, D, BANK):
                 out_bank = psum_out.tile([P, BANK], F32)
@@ -217,18 +216,16 @@ def tile_llamamlp_halfwaygin_pa_t_kernel(tc, h_inter, adjacency, Wd, eps, alpha,
                 )
                 banks.append((d0, out_bank))
             for d0, out_bank in banks:
-                nc.scalar.copy(out=out_sb[:, e, d0 : d0 + BANK], in_=out_bank[:])
-            if e == 1:
-                nc.scalar.dma_start(
-                    out=out[b, u * 2 * P : (u + 1) * 2 * P, :].rearrange("(p e) d -> p (e d)", e=2),
-                    in_=out_sb[:].rearrange("p e d -> p (e d)"),
-                )
+                nc.scalar.copy(out=out_sb[:, d0 : d0 + BANK], in_=out_bank[:])
+            nc.sync.dma_start(
+                out=out[b].rearrange("(u p e) d -> u e p d", u=HALVES, e=2)[u, e], in_=out_sb[:]
+            )
 
-        load_step(0)
-        load_step(1)
+        for s in range(H):
+            load_step(s)
         wd_raw = consts.tile([P, PACK, D], BF16)
         load(wd_raw, Wd)
-        for s in range(2, PREFETCH):
+        for s in range(H, PREFETCH):
             load_step(s)
 
         ident = consts.tile([P, P], F32)
@@ -257,9 +254,12 @@ def tile_llamamlp_halfwaygin_pa_t_kernel(tc, h_inter, adjacency, Wd, eps, alpha,
                 a_grouped = a_transpose_and_copy(s)
             if live(j):
                 g_bank = g_transpose(j)
-                g_copy(j, g_bank)
             if 0 <= piece < WD_PIECES:
                 wd_regroup(piece)
+            if live(s - 2):
+                combine(s - 2)
+            if live(j):
+                g_copy(j, g_bank)
             if live(s + 1):
                 h_regroup(s + 1)
             if live(s):
@@ -270,10 +270,9 @@ def tile_llamamlp_halfwaygin_pa_t_kernel(tc, h_inter, adjacency, Wd, eps, alpha,
                 g_quantise(j)
             if 0 <= piece - 1 < WD_PIECES:
                 wd_quantise(piece - 1)
-            if live(s - 1):
-                agg = first_matmul(s - 1)
-                combine(s - 1, agg)
             if live(s + 1):
                 h_quantise(s + 1)
+            if live(s - 1):
+                first_matmul(s - 1)
             if live(j - 1):
                 second_matmul_and_store(j - 1)

@@ -58,7 +58,7 @@ def tile_llamamlp_halfwaygin_pa_t_kernel(tc, h_inter, adjacency, Wd, eps, alpha,
         def load_step(s):
             b, n = divmod(s, H)
             a_raw = a_pool.tile([P, PACK, S], BF16)
-            load(a_raw, adjacency[b, n])
+            nc.sync.dma_start(out=a_raw[:], in_=adjacency[b, n].rearrange("(p t) w -> p t w", t=PACK))
             a_raw_of[s] = a_raw
             if n == 0:
                 h_raw = h_pool.tile([P, PACK, I], BF16)
@@ -114,15 +114,15 @@ def tile_llamamlp_halfwaygin_pa_t_kernel(tc, h_inter, adjacency, Wd, eps, alpha,
             a_words = a_grouped[:].bitcast(F32)
             sets_a_bank = BANK // (HALVES * P)
             banks = []
-            for first_set in range(0, PACK, sets_a_bank):
-                a_bank = psum_t.tile([P, HALVES, sets_a_bank, P], F32, tag="transposed")
-                for i in range(sets_a_bank):
-                    transpose_row_set(a_bank[:, :, i, :], a_raw, first_set + i)
-                banks.append((first_set, a_bank))
-            for first_set, a_bank in banks:
+            for e in range(2):
+                a_bank = psum_t.tile([P, sets_a_bank, HALVES, P], F32, tag="transposed")
+                for a in range(sets_a_bank):
+                    transpose_row_set(a_bank[:, a, :, :], a_raw, 2 * a + e)
+                banks.append((e, a_bank))
+            for e, a_bank in banks:
                 nc.scalar.copy(
-                    out=a_words[:, first_set * P : (first_set + sets_a_bank) * P, :],
-                    in_=a_bank[:].rearrange("q u i p -> q (i p) u"),
+                    out=a_words[:, e * 2 * P : (e + 1) * 2 * P, :].rearrange("q (p a) u -> q p (a u)", a=sets_a_bank),
+                    in_=a_bank[:].rearrange("q a u p -> q p (a u)"),
                 )
             return a_grouped
 
@@ -137,7 +137,8 @@ def tile_llamamlp_halfwaygin_pa_t_kernel(tc, h_inter, adjacency, Wd, eps, alpha,
             h_codes, h_scales = h_codes_of[s]
             agg = psum_agg.tile([P, PACK, HD], F32)
             for t in range(PACK):
-                row_set = slice(t * P, (t + 1) * P)
+                u, e = divmod(t, 2)
+                row_set = slice((2 * e + u) * P, (2 * e + u + 1) * P)
                 nc.tensor.matmul_mx(
                     out=agg[:, t, :],
                     lhsT=a_codes[:, row_set].bitcast(FP8X4),

@@ -20,7 +20,7 @@ HALVES = 2
 FLOPS = 2 * B * H * S * S * HD + 2 * B * S * I * D
 
 STEPS = B * H
-PREFETCH = 12
+PREFETCH = 10
 G_LAG = 6
 WD_PIECES = 4
 WD_FIRST_STEP = 2
@@ -35,7 +35,7 @@ def tile_llamamlp_halfwaygin_pa_t_kernel(tc, h_inter, adjacency, Wd, eps, alpha,
         h_pool = ctx.enter_context(tc.tile_pool(name="h_pool", bufs=PREFETCH // H + 2))
         work = ctx.enter_context(tc.tile_pool(name="work", bufs=3))
         scaled_pool = ctx.enter_context(tc.tile_pool(name="scaled_pool", bufs=PREFETCH + H))
-        out_pool = ctx.enter_context(tc.tile_pool(name="out_pool", bufs=6))
+        out_pool = ctx.enter_context(tc.tile_pool(name="out_pool", bufs=10))
         psum_t = ctx.enter_context(tc.psum_pool(name="psum_t", bufs=3))
         psum_agg = ctx.enter_context(tc.psum_pool(name="psum_agg", bufs=2))
         psum_out = ctx.enter_context(tc.psum_pool(name="psum_out", bufs=3))

@@ -23,7 +23,9 @@ STEPS = B * H
 PREFETCH = 10
 G_LAG = 6
 WD_PIECES = 4
-WD_FIRST_STEP = 2
+WD_FIRST_STEP = 3
+VECTOR_ROW_SET = 1
+VECTOR_FROM = 26
 
 
 def tile_llamamlp_halfwaygin_pa_t_kernel(tc, h_inter, adjacency, Wd, eps, alpha, out):
@@ -34,13 +36,13 @@ def tile_llamamlp_halfwaygin_pa_t_kernel(tc, h_inter, adjacency, Wd, eps, alpha,
         a_pool = ctx.enter_context(tc.tile_pool(name="a_pool", bufs=PREFETCH + 1))
         h_pool = ctx.enter_context(tc.tile_pool(name="h_pool", bufs=PREFETCH // H + 2))
         work = ctx.enter_context(tc.tile_pool(name="work", bufs=3))
-        scaled_pool = ctx.enter_context(tc.tile_pool(name="scaled_pool", bufs=PREFETCH + H))
+        scaled_pool = ctx.enter_context(tc.tile_pool(name="scaled_pool", bufs=3))
         out_pool = ctx.enter_context(tc.tile_pool(name="out_pool", bufs=10))
         psum_t = ctx.enter_context(tc.psum_pool(name="psum_t", bufs=3))
         psum_agg = ctx.enter_context(tc.psum_pool(name="psum_agg", bufs=2))
         psum_out = ctx.enter_context(tc.psum_pool(name="psum_out", bufs=3))
 
-        a_raw_of, h_raw_of = {}, {}
+        a_raw_of, h_raw_of, a_grouped_of = {}, {}, {}
         a_codes_of, h_codes_of, g_codes_of = {}, {}, {}
         h_grouped_of, h_scaled_of, agg_of, g_of, g_grouped_of, wd_grouped_of = {}, {}, {}, {}, {}, {}
 
@@ -76,8 +78,9 @@ def tile_llamamlp_halfwaygin_pa_t_kernel(tc, h_inter, adjacency, Wd, eps, alpha,
             )
 
         def h_regroup(s):
-            h_grouped = work.tile([P, HD, PACK], BF16, align_bytes=64)
-            regroup(nc.vector.tensor_copy, h_grouped[:], h_raw_of[s // H][:, :, head_columns(s)])
+            h_grouped = work.tile([P, 2 * HD, PACK], BF16, align_bytes=64)
+            n = s % H
+            regroup(nc.vector.tensor_copy, h_grouped[:], h_raw_of[s // H][:, :, n * HD : (n + 2) * HD])
             h_grouped_of[s] = h_grouped
 
         def h_scale(s):
@@ -98,38 +101,42 @@ def tile_llamamlp_halfwaygin_pa_t_kernel(tc, h_inter, adjacency, Wd, eps, alpha,
             )
 
         def h_quantise(s):
-            h_codes = work.tile([P, HD], U32, align_bytes=64)
-            h_scales = work.tile([P, HD], U8, align_bytes=64)
+            h_codes = work.tile([P, 2 * HD], U32, align_bytes=64)
+            h_scales = work.tile([P, 2 * HD], U8, align_bytes=64)
             quantise(h_grouped_of[s][:], h_codes[:], h_scales[:])
-            h_codes_of[s] = (h_codes, h_scales)
+            for i in range(2):
+                columns = slice(i * HD, (i + 1) * HD)
+                h_codes_of[s + i] = (h_codes[:, columns], h_scales[:, columns])
 
         def transpose_row_set(bank_part, raw, t):
             words = raw[:].bitcast(F32)
             for u in range(HALVES):
                 nc.tensor.transpose(bank_part[:, u, :], words[:, t, u * P : (u + 1) * P], ident[:])
 
-        def a_transpose_and_copy(s):
+        def a_transpose(s):
             a_raw = a_raw_of[s]
-            a_grouped = work.tile([P, S, PACK], BF16, align_bytes=64)
-            a_words = a_grouped[:].bitcast(F32)
-            sets_a_bank = BANK // (HALVES * P)
             banks = []
             for e in range(2):
-                a_bank = psum_t.tile([P, sets_a_bank, HALVES, P], F32, tag="transposed")
-                for a in range(sets_a_bank):
+                a_bank = psum_t.tile([P, 2, HALVES, P], F32, tag="transposed")
+                for a in range(2):
                     transpose_row_set(a_bank[:, a, :, :], a_raw, 2 * a + e)
                 banks.append((e, a_bank))
+            return banks
+
+        def a_copy(s, banks):
+            a_grouped = work.tile([P, S, PACK], BF16, align_bytes=64)
+            a_words = a_grouped[:].bitcast(F32)
             for e, a_bank in banks:
                 nc.scalar.copy(
-                    out=a_words[:, e * 2 * P : (e + 1) * 2 * P, :].rearrange("q (p a) u -> q p (a u)", a=sets_a_bank),
+                    out=a_words[:, e * 2 * P : (e + 1) * 2 * P, :].rearrange("q (p a) u -> q p (a u)", a=2),
                     in_=a_bank[:].rearrange("q a u p -> q p (a u)"),
                 )
-            return a_grouped
+            a_grouped_of[s] = a_grouped
 
-        def a_quantise(s, a_grouped):
+        def a_quantise(s):
             a_codes = work.tile([P, S], U32, align_bytes=64)
             a_scales = work.tile([P, S], U8, align_bytes=64)
-            quantise(a_grouped[:], a_codes[:], a_scales[:])
+            quantise(a_grouped_of[s][:], a_codes[:], a_scales[:])
             a_codes_of[s] = (a_codes, a_scales)
 
         def first_matmul(s):
@@ -143,8 +150,8 @@ def tile_llamamlp_halfwaygin_pa_t_kernel(tc, h_inter, adjacency, Wd, eps, alpha,
                     out=agg[:, t, :],
                     lhsT=a_codes[:, row_set].bitcast(FP8X4),
                     lhsT_scale=a_scales[:, row_set],
-                    rhs=h_codes[:].bitcast(FP8X4),
-                    rhs_scale=h_scales[:],
+                    rhs=h_codes.bitcast(FP8X4),
+                    rhs_scale=h_scales,
                     start=True,
                     stop=True,
                 )
@@ -216,8 +223,11 @@ def tile_llamamlp_halfwaygin_pa_t_kernel(tc, h_inter, adjacency, Wd, eps, alpha,
                     stop=True,
                 )
                 banks.append((d0, out_bank))
-            for d0, out_bank in banks:
-                nc.scalar.copy(out=out_sb[:, d0 : d0 + BANK], in_=out_bank[:])
+            for i, (d0, out_bank) in enumerate(banks):
+                if i == 1 and (t == VECTOR_ROW_SET or j >= VECTOR_FROM):
+                    nc.vector.tensor_copy(out=out_sb[:, d0 : d0 + BANK], in_=out_bank[:])
+                else:
+                    nc.scalar.copy(out=out_sb[:, d0 : d0 + BANK], in_=out_bank[:])
             nc.sync.dma_start(
                 out=out[b].rearrange("(u p e) d -> u e p d", u=HALVES, e=2)[u, e], in_=out_sb[:]
             )
@@ -242,38 +252,38 @@ def tile_llamamlp_halfwaygin_pa_t_kernel(tc, h_inter, adjacency, Wd, eps, alpha,
         wd_codes = consts.tile([P, D], U32, align_bytes=64)
         wd_scales = consts.tile([P, D], U8, align_bytes=64)
 
-        h_regroup(0)
         h_scale(0)
-        h_quantise(0)
 
-        for s in range(STEPS + G_LAG + 1):
+        for s in range(STEPS + G_LAG + 2):
             j = s - G_LAG
             piece = s - WD_FIRST_STEP
             if live(s + PREFETCH):
                 load_step(s + PREFETCH)
             if live(s):
-                a_grouped = a_transpose_and_copy(s)
+                a_banks = a_transpose(s)
             if live(j):
                 g_bank = g_transpose(j)
+            if live(s - 2):
+                first_matmul(s - 2)
+            if live(s):
+                a_copy(s, a_banks)
             if 0 <= piece < WD_PIECES:
                 wd_regroup(piece)
-            if live(s - 2):
-                combine(s - 2)
             if live(j):
                 g_copy(j, g_bank)
-            if live(s + 1):
-                h_regroup(s + 1)
-            if live(s):
-                a_quantise(s, a_grouped)
-            if live(s + 1):
-                h_scale(s + 1)
-            if live(j):
-                g_quantise(j)
+            if live(s) and s % 2 == 0:
+                h_regroup(s)
+            if live(s) and s % 2 == 1:
+                h_quantise(s - 1)
+            if live(j - 1):
+                g_quantise(j - 1)
             if 0 <= piece - 1 < WD_PIECES:
                 wd_quantise(piece - 1)
+            if live(s - 2):
+                combine(s - 2)
+            if live(j - 2):
+                second_matmul_and_store(j - 2)
+            if live(s):
+                a_quantise(s)
             if live(s + 1):
-                h_quantise(s + 1)
-            if live(s - 1):
-                first_matmul(s - 1)
-            if live(j - 1):
-                second_matmul_and_store(j - 1)
+                h_scale(s + 1)

@@ -24,8 +24,6 @@ PREFETCH = 10
 G_LAG = 6
 WD_PIECES = 4
 WD_FIRST_STEP = 3
-VECTOR_ROW_SET = 1
-VECTOR_FROM = 26
 
 
 def tile_llamamlp_halfwaygin_pa_t_kernel(tc, h_inter, adjacency, Wd, eps, alpha, out):
@@ -39,8 +37,8 @@ def tile_llamamlp_halfwaygin_pa_t_kernel(tc, h_inter, adjacency, Wd, eps, alpha,
         scaled_pool = ctx.enter_context(tc.tile_pool(name="scaled_pool", bufs=3))
         out_pool = ctx.enter_context(tc.tile_pool(name="out_pool", bufs=10))
         psum_t = ctx.enter_context(tc.psum_pool(name="psum_t", bufs=3))
-        psum_agg = ctx.enter_context(tc.psum_pool(name="psum_agg", bufs=2))
-        psum_out = ctx.enter_context(tc.psum_pool(name="psum_out", bufs=3))
+        psum_agg = ctx.enter_context(tc.psum_pool(name="psum_agg", bufs=1))
+        psum_out = ctx.enter_context(tc.psum_pool(name="psum_out", bufs=4))
 
         a_raw_of, h_raw_of, a_grouped_of = {}, {}, {}
         a_codes_of, h_codes_of, g_codes_of = {}, {}, {}
@@ -78,9 +76,8 @@ def tile_llamamlp_halfwaygin_pa_t_kernel(tc, h_inter, adjacency, Wd, eps, alpha,
             )
 
         def h_regroup(s):
-            h_grouped = work.tile([P, 2 * HD, PACK], BF16, align_bytes=64)
-            n = s % H
-            regroup(nc.vector.tensor_copy, h_grouped[:], h_raw_of[s // H][:, :, n * HD : (n + 2) * HD])
+            h_grouped = work.tile([P, HD, PACK], BF16, align_bytes=64)
+            regroup(nc.vector.tensor_copy, h_grouped[:], h_raw_of[s // H][:, :, head_columns(s)])
             h_grouped_of[s] = h_grouped
 
         def h_scale(s):
@@ -101,12 +98,10 @@ def tile_llamamlp_halfwaygin_pa_t_kernel(tc, h_inter, adjacency, Wd, eps, alpha,
             )
 
         def h_quantise(s):
-            h_codes = work.tile([P, 2 * HD], U32, align_bytes=64)
-            h_scales = work.tile([P, 2 * HD], U8, align_bytes=64)
+            h_codes = work.tile([P, HD], U32, align_bytes=64)
+            h_scales = work.tile([P, HD], U8, align_bytes=64)
             quantise(h_grouped_of[s][:], h_codes[:], h_scales[:])
-            for i in range(2):
-                columns = slice(i * HD, (i + 1) * HD)
-                h_codes_of[s + i] = (h_codes[:, columns], h_scales[:, columns])
+            h_codes_of[s] = (h_codes, h_scales)
 
         def transpose_row_set(bank_part, raw, t):
             words = raw[:].bitcast(F32)
@@ -150,8 +145,8 @@ def tile_llamamlp_halfwaygin_pa_t_kernel(tc, h_inter, adjacency, Wd, eps, alpha,
                     out=agg[:, t, :],
                     lhsT=a_codes[:, row_set].bitcast(FP8X4),
                     lhsT_scale=a_scales[:, row_set],
-                    rhs=h_codes.bitcast(FP8X4),
-                    rhs_scale=h_scales,
+                    rhs=h_codes[:].bitcast(FP8X4),
+                    rhs_scale=h_scales[:],
                     start=True,
                     stop=True,
                 )
@@ -223,11 +218,8 @@ def tile_llamamlp_halfwaygin_pa_t_kernel(tc, h_inter, adjacency, Wd, eps, alpha,
                     stop=True,
                 )
                 banks.append((d0, out_bank))
-            for i, (d0, out_bank) in enumerate(banks):
-                if i == 1 and (t == VECTOR_ROW_SET or j >= VECTOR_FROM):
-                    nc.vector.tensor_copy(out=out_sb[:, d0 : d0 + BANK], in_=out_bank[:])
-                else:
-                    nc.scalar.copy(out=out_sb[:, d0 : d0 + BANK], in_=out_bank[:])
+            for d0, out_bank in banks:
+                nc.scalar.copy(out=out_sb[:, d0 : d0 + BANK], in_=out_bank[:])
             nc.sync.dma_start(
                 out=out[b].rearrange("(u p e) d -> u e p d", u=HALVES, e=2)[u, e], in_=out_sb[:]
             )
@@ -254,7 +246,7 @@ def tile_llamamlp_halfwaygin_pa_t_kernel(tc, h_inter, adjacency, Wd, eps, alpha,
 
         h_scale(0)
 
-        for s in range(STEPS + G_LAG + 2):
+        for s in range(STEPS + G_LAG + 1):
             j = s - G_LAG
             piece = s - WD_FIRST_STEP
             if live(s + PREFETCH):
@@ -269,21 +261,20 @@ def tile_llamamlp_halfwaygin_pa_t_kernel(tc, h_inter, adjacency, Wd, eps, alpha,
                 a_copy(s, a_banks)
             if 0 <= piece < WD_PIECES:
                 wd_regroup(piece)
-            if live(j):
-                g_copy(j, g_bank)
-            if live(s) and s % 2 == 0:
-                h_regroup(s)
-            if live(s) and s % 2 == 1:
-                h_quantise(s - 1)
-            if live(j - 1):
-                g_quantise(j - 1)
+            if live(s - 1):
+                h_regroup(s - 1)
             if 0 <= piece - 1 < WD_PIECES:
                 wd_quantise(piece - 1)
+            if live(s - 1):
+                a_quantise(s - 1)
+                h_quantise(s - 1)
+            if live(j):
+                g_copy(j, g_bank)
             if live(s - 2):
                 combine(s - 2)
-            if live(j - 2):
-                second_matmul_and_store(j - 2)
-            if live(s):
-                a_quantise(s)
+            if live(j):
+                g_quantise(j)
             if live(s + 1):
                 h_scale(s + 1)
+            if live(j - 1):
+                second_matmul_and_store(j - 1)

@@ -22,6 +22,7 @@ FLOPS = 2 * B * H * S * S * HD + 2 * B * S * I * D
 STEPS = B * H
 PREFETCH = 10
 G_LAG = 6
+SINGLE_STORES_FROM = 24
 WD_PIECES = 4
 WD_FIRST_STEP = 3
 
@@ -31,16 +32,16 @@ def tile_llamamlp_halfwaygin_pa_t_kernel(tc, h_inter, adjacency, Wd, eps, alpha,
     with ExitStack() as ctx:
         ctx.enter_context(tc.manual_schedule())
         consts = ctx.enter_context(tc.tile_pool(name="consts", bufs=1))
-        a_pool = ctx.enter_context(tc.tile_pool(name="a_pool", bufs=PREFETCH + 1))
+        a_pool = ctx.enter_context(tc.tile_pool(name="a_pool", bufs=PREFETCH + 2))
         h_pool = ctx.enter_context(tc.tile_pool(name="h_pool", bufs=PREFETCH // H + 2))
         work = ctx.enter_context(tc.tile_pool(name="work", bufs=3))
         scaled_pool = ctx.enter_context(tc.tile_pool(name="scaled_pool", bufs=3))
-        out_pool = ctx.enter_context(tc.tile_pool(name="out_pool", bufs=10))
+        out_pool = ctx.enter_context(tc.tile_pool(name="out_pool", bufs=6))
         psum_t = ctx.enter_context(tc.psum_pool(name="psum_t", bufs=3))
         psum_agg = ctx.enter_context(tc.psum_pool(name="psum_agg", bufs=1))
         psum_out = ctx.enter_context(tc.psum_pool(name="psum_out", bufs=4))
 
-        a_raw_of, h_raw_of, a_grouped_of = {}, {}, {}
+        a_raw_of, h_raw_of, a_grouped_of, out_sb_of = {}, {}, {}, {}
         a_codes_of, h_codes_of, g_codes_of = {}, {}, {}
         h_grouped_of, h_scaled_of, agg_of, g_of, g_grouped_of, wd_grouped_of = {}, {}, {}, {}, {}, {}
 
@@ -204,7 +205,9 @@ def tile_llamamlp_halfwaygin_pa_t_kernel(tc, h_inter, adjacency, Wd, eps, alpha,
             b, t = divmod(j, PACK)
             u, e = divmod(t, 2)
             g_codes, g_scales = g_codes_of[j]
-            out_sb = out_pool.tile([P, D], F32)
+            if e == 0:
+                out_sb_of[j // 2] = out_pool.tile([P, 2, D], F32, name="out_sb")
+            out_sb = out_sb_of[j // 2]
             banks = []
             for d0 in range(0, D, BANK):
                 out_bank = psum_out.tile([P, BANK], F32)
@@ -219,10 +222,12 @@ def tile_llamamlp_halfwaygin_pa_t_kernel(tc, h_inter, adjacency, Wd, eps, alpha,
                 )
                 banks.append((d0, out_bank))
             for d0, out_bank in banks:
-                nc.scalar.copy(out=out_sb[:, d0 : d0 + BANK], in_=out_bank[:])
-            nc.sync.dma_start(
-                out=out[b].rearrange("(u p e) d -> u e p d", u=HALVES, e=2)[u, e], in_=out_sb[:]
-            )
+                nc.scalar.copy(out=out_sb[:, e, d0 : d0 + BANK], in_=out_bank[:])
+            rows = out[b].rearrange("(u p e) d -> u p e d", u=HALVES, e=2)[u]
+            if j >= SINGLE_STORES_FROM:
+                nc.sync.dma_start(out=rows[:, e, :], in_=out_sb[:, e, :])
+            elif e == 1:
+                nc.sync.dma_start(out=rows, in_=out_sb[:])
 
         for s in range(H):
             load_step(s)
@@ -239,8 +244,10 @@ def tile_llamamlp_halfwaygin_pa_t_kernel(tc, h_inter, adjacency, Wd, eps, alpha,
         nc.scalar.dma_start(out=alpha_bf16[:], in_=alpha.partition_broadcast(P))
         one_plus_eps = consts.tile([P, H], F32)
         alpha_f32 = consts.tile([P, H], F32)
-        nc.vector.tensor_scalar_add(out=one_plus_eps[:], in0=eps_bf16[:], scalar1=1.0)
-        nc.vector.tensor_copy(out=alpha_f32[:], in_=alpha_bf16[:])
+        nc.gpsimd.tensor_scalar(
+            out=one_plus_eps[:], in0=eps_bf16[:], scalar1=1.0, scalar2=None, op0=ADD
+        )
+        nc.gpsimd.tensor_copy(out=alpha_f32[:], in_=alpha_bf16[:])
         wd_codes = consts.tile([P, D], U32, align_bytes=64)
         wd_scales = consts.tile([P, D], U8, align_bytes=64)
 
@@ -249,8 +256,10 @@ def tile_llamamlp_halfwaygin_pa_t_kernel(tc, h_inter, adjacency, Wd, eps, alpha,
         for s in range(STEPS + G_LAG + 1):
             j = s - G_LAG
             piece = s - WD_FIRST_STEP
-            if live(s + PREFETCH):
-                load_step(s + PREFETCH)
+            if s % 2 == 0:
+                for later in (s + PREFETCH, s + PREFETCH + 1):
+                    if live(later):
+                        load_step(later)
             if live(s):
                 a_banks = a_transpose(s)
             if live(j):

from contextlib import ExitStack

import concourse.mybir as mybir
from concourse.masks import make_identity

BF16 = mybir.dt.bfloat16
F32 = mybir.dt.float32
U32 = mybir.dt.uint32
U8 = mybir.dt.uint8
FP8X4 = mybir.dt.float8_e4m3fn_x4
MULT = mybir.AluOpType.mult
ADD = mybir.AluOpType.add

B, S, I, H, HD, D = 8, 512, 512, 4, 128, 1024
P = 128
PACK = 4
BANK = 512
HALVES = 2

FLOPS = 2 * B * H * S * S * HD + 2 * B * S * I * D

STEPS = B * H
PREFETCH = 10
G_LAG = 6
SINGLE_STORES_FROM = 24
WD_PIECES = 4
WD_FIRST_STEP = 3


def tile_llamamlp_halfwaygin_pa_t_kernel(tc, h_inter, adjacency, Wd, eps, alpha, out):
    nc = tc.nc
    with ExitStack() as ctx:
        ctx.enter_context(tc.manual_schedule())
        consts = ctx.enter_context(tc.tile_pool(name="consts", bufs=1))
        a_pool = ctx.enter_context(tc.tile_pool(name="a_pool", bufs=PREFETCH + 2))
        h_pool = ctx.enter_context(tc.tile_pool(name="h_pool", bufs=PREFETCH // H + 2))
        work = ctx.enter_context(tc.tile_pool(name="work", bufs=3))
        scaled_pool = ctx.enter_context(tc.tile_pool(name="scaled_pool", bufs=3))
        out_pool = ctx.enter_context(tc.tile_pool(name="out_pool", bufs=6))
        psum_t = ctx.enter_context(tc.psum_pool(name="psum_t", bufs=3))
        psum_agg = ctx.enter_context(tc.psum_pool(name="psum_agg", bufs=1))
        psum_out = ctx.enter_context(tc.psum_pool(name="psum_out", bufs=4))

        a_raw_of, h_raw_of, a_grouped_of, out_sb_of = {}, {}, {}, {}
        a_codes_of, h_codes_of, g_codes_of = {}, {}, {}
        h_grouped_of, h_scaled_of, agg_of, g_of, g_grouped_of, wd_grouped_of = {}, {}, {}, {}, {}, {}

        def live(step):
            return 0 <= step < STEPS

        def in_place_order(rows):
            return rows.rearrange("(u p e) w -> p u (e w)", u=HALVES, e=2)

        def load(tile, rows):
            nc.sync.dma_start(
                out=tile[:].rearrange("p (u e) w -> p u (e w)", u=HALVES), in_=in_place_order(rows)
            )

        def load_step(s):
            b, n = divmod(s, H)
            a_raw = a_pool.tile([P, PACK, S], BF16)
            nc.sync.dma_start(out=a_raw[:], in_=adjacency[b, n].rearrange("(p t) w -> p t w", t=PACK))
            a_raw_of[s] = a_raw
            if n == 0:
                h_raw = h_pool.tile([P, PACK, I], BF16)
                load(h_raw, h_inter[b])
                h_raw_of[b] = h_raw

        def head_columns(s):
            n = s % H
            return slice(n * HD, (n + 1) * HD)

        def regroup(engine_copy, grouped, raw):
            engine_copy(
                out=grouped.rearrange("p (c i) t -> p c t i", i=4),
                in_=raw.rearrange("p t (c i) -> p c t i", i=4),
            )

        def h_regroup(s):
            h_grouped = work.tile([P, HD, PACK], BF16, align_bytes=64)
            regroup(nc.vector.tensor_copy, h_grouped[:], h_raw_of[s // H][:, :, head_columns(s)])
            h_grouped_of[s] = h_grouped

        def h_scale(s):
            h_scaled = scaled_pool.tile([P, PACK, HD], F32)
            nc.gpsimd.tensor_scalar(
                out=h_scaled[:],
                in0=h_raw_of[s // H][:, :, head_columns(s)],
                scalar1=one_plus_eps[:, s % H : s % H + 1],
                scalar2=0.0,
                op0=MULT,
                op1=ADD,
            )
            h_scaled_of[s] = h_scaled

        def quantise(grouped, codes, scales):
            nc.vector.quantize_mx(
                out=codes.bitcast(FP8X4), scales=scales, in_=grouped.rearrange("p c t -> p (c t)")
            )

        def h_quantise(s):
            h_codes = work.tile([P, HD], U32, align_bytes=64)
            h_scales = work.tile([P, HD], U8, align_bytes=64)
            quantise(h_grouped_of[s][:], h_codes[:], h_scales[:])
            h_codes_of[s] = (h_codes, h_scales)

        def transpose_row_set(bank_part, raw, t):
            words = raw[:].bitcast(F32)
            for u in range(HALVES):
                nc.tensor.transpose(bank_part[:, u, :], words[:, t, u * P : (u + 1) * P], ident[:])

        def a_transpose(s):
            a_raw = a_raw_of[s]
            banks = []
            for e in range(2):
                a_bank = psum_t.tile([P, 2, HALVES, P], F32, tag="transposed")
                for a in range(2):
                    transpose_row_set(a_bank[:, a, :, :], a_raw, 2 * a + e)
                banks.append((e, a_bank))
            return banks

        def a_copy(s, banks):
            a_grouped = work.tile([P, S, PACK], BF16, align_bytes=64)
            a_words = a_grouped[:].bitcast(F32)
            for e, a_bank in banks:
                nc.scalar.copy(
                    out=a_words[:, e * 2 * P : (e + 1) * 2 * P, :].rearrange("q (p a) u -> q p (a u)", a=2),
                    in_=a_bank[:].rearrange("q a u p -> q p (a u)"),
                )
            a_grouped_of[s] = a_grouped

        def a_quantise(s):
            a_codes = work.tile([P, S], U32, align_bytes=64)
            a_scales = work.tile([P, S], U8, align_bytes=64)
            quantise(a_grouped_of[s][:], a_codes[:], a_scales[:])
            a_codes_of[s] = (a_codes, a_scales)

        def first_matmul(s):
            a_codes, a_scales = a_codes_of[s]
            h_codes, h_scales = h_codes_of[s]
            agg = psum_agg.tile([P, PACK, HD], F32)
            for t in range(PACK):
                u, e = divmod(t, 2)
                row_set = slice((2 * e + u) * P, (2 * e + u + 1) * P)
                nc.tensor.matmul_mx(
                    out=agg[:, t, :],
                    lhsT=a_codes[:, row_set].bitcast(FP8X4),
                    lhsT_scale=a_scales[:, row_set],
                    rhs=h_codes[:].bitcast(FP8X4),
                    rhs_scale=h_scales[:],
                    start=True,
                    stop=True,
                )
            agg_of[s] = agg

        def combine(s):
            b, n = divmod(s, H)
            if n == 0:
                g_new = work.tile([P, PACK, I], BF16)
                g_of[b] = g_new
            nc.vector.scalar_tensor_tensor(
                out=g_of[b][:, :, head_columns(s)],
                in0=agg_of[s][:],
                scalar=alpha_f32[:, n : n + 1],
                in1=h_scaled_of[s][:],
                op0=MULT,
                op1=ADD,
            )

        def g_transpose(j):
            b, t = divmod(j, PACK)
            g_bank = psum_t.tile([P, HALVES, P], F32, tag="transposed")
            transpose_row_set(g_bank[:], g_of[b], t)
            return g_bank

        def g_copy(j, g_bank):
            g_grouped = work.tile([P, P, PACK], BF16, align_bytes=64)
            nc.vector.tensor_copy(
                out=g_grouped[:].bitcast(F32), in_=g_bank[:].rearrange("q u p -> q p u")
            )
            g_grouped_of[j] = g_grouped

        def g_quantise(j):
            g_codes = work.tile([P, P], U32, align_bytes=64)
            g_scales = work.tile([P, P], U8, align_bytes=64)
            quantise(g_grouped_of[j][:], g_codes[:], g_scales[:])
            g_codes_of[j] = (g_codes, g_scales)

        def wd_columns(piece):
            return slice(piece * (D // WD_PIECES), (piece + 1) * (D // WD_PIECES))

        def wd_regroup(piece):
            wd_grouped = work.tile([P, D // WD_PIECES, PACK], BF16, align_bytes=64)
            regroup(nc.scalar.copy, wd_grouped[:], wd_raw[:, :, wd_columns(piece)])
            wd_grouped_of[piece] = wd_grouped

        def wd_quantise(piece):
            quantise(
                wd_grouped_of[piece][:],
                wd_codes[:, wd_columns(piece)],
                wd_scales[:, wd_columns(piece)],
            )

        def second_matmul_and_store(j):
            b, t = divmod(j, PACK)
            u, e = divmod(t, 2)
            g_codes, g_scales = g_codes_of[j]
            if e == 0:
                out_sb_of[j // 2] = out_pool.tile([P, 2, D], F32, name="out_sb")
            out_sb = out_sb_of[j // 2]
            banks = []
            for d0 in range(0, D, BANK):
                out_bank = psum_out.tile([P, BANK], F32)
                nc.tensor.matmul_mx(
                    out=out_bank[:],
                    lhsT=g_codes[:].bitcast(FP8X4),
                    lhsT_scale=g_scales[:],
                    rhs=wd_codes[:, d0 : d0 + BANK].bitcast(FP8X4),
                    rhs_scale=wd_scales[:, d0 : d0 + BANK],
                    start=True,
                    stop=True,
                )
                banks.append((d0, out_bank))
            for d0, out_bank in banks:
                nc.scalar.copy(out=out_sb[:, e, d0 : d0 + BANK], in_=out_bank[:])
            rows = out[b].rearrange("(u p e) d -> u p e d", u=HALVES, e=2)[u]
            if j >= SINGLE_STORES_FROM:
                nc.sync.dma_start(out=rows[:, e, :], in_=out_sb[:, e, :])
            elif e == 1:
                nc.sync.dma_start(out=rows, in_=out_sb[:])

        for s in range(H):
            load_step(s)
        wd_raw = consts.tile([P, PACK, D], BF16)
        load(wd_raw, Wd)
        for s in range(H, PREFETCH):
            load_step(s)

        ident = consts.tile([P, P], F32)
        make_identity(nc, ident[:])
        eps_bf16 = consts.tile([P, H], BF16)
        alpha_bf16 = consts.tile([P, H], BF16)
        nc.scalar.dma_start(out=eps_bf16[:], in_=eps.partition_broadcast(P))
        nc.scalar.dma_start(out=alpha_bf16[:], in_=alpha.partition_broadcast(P))
        one_plus_eps = consts.tile([P, H], F32)
        alpha_f32 = consts.tile([P, H], F32)
        nc.gpsimd.tensor_scalar(
            out=one_plus_eps[:], in0=eps_bf16[:], scalar1=1.0, scalar2=None, op0=ADD
        )
        nc.gpsimd.tensor_copy(out=alpha_f32[:], in_=alpha_bf16[:])
        wd_codes = consts.tile([P, D], U32, align_bytes=64)
        wd_scales = consts.tile([P, D], U8, align_bytes=64)

        h_scale(0)

        for s in range(STEPS + G_LAG + 1):
            j = s - G_LAG
            piece = s - WD_FIRST_STEP
            if s % 2 == 0:
                for later in (s + PREFETCH, s + PREFETCH + 1):
                    if live(later):
                        load_step(later)
            if live(s):
                a_banks = a_transpose(s)
            if live(j):
                g_bank = g_transpose(j)
            if live(s - 2):
                first_matmul(s - 2)
            if live(s):
                a_copy(s, a_banks)
            if 0 <= piece < WD_PIECES:
                wd_regroup(piece)
            if live(s - 1):
                h_regroup(s - 1)
            if 0 <= piece - 1 < WD_PIECES:
                wd_quantise(piece - 1)
            if live(s - 1):
                a_quantise(s - 1)
                h_quantise(s - 1)
            if live(j):
                g_copy(j, g_bank)
            if live(s - 2):
                combine(s - 2)
            if live(j):
                g_quantise(j)
            if live(s + 1):
                h_scale(s + 1)
            if live(j - 1):
                second_matmul_and_store(j - 1)
